import numpy as np
import ml_dtypes


def mxq(x, axis, fmt="e4m3"):
    dtype, down = {"e4m3": (ml_dtypes.float8_e4m3fn, 7), "e5m2": (ml_dtypes.float8_e5m2, 14)}[fmt]
    v = np.moveaxis(np.asarray(x, np.float32).astype(ml_dtypes.bfloat16).astype(np.float64), axis, -1)
    blocks = v.reshape(v.shape[:-1] + (-1, 32))
    amax = np.abs(blocks).max(-1, keepdims=True)
    byte = np.maximum(np.where(amax > 0, np.frexp(amax)[1] - 1 + 127, 0) - down, 1)
    scale = np.exp2(byte - 127.0)
    codes = (blocks / scale).astype(np.float32).astype(dtype).astype(np.float64)
    return np.moveaxis((codes * scale).reshape(v.shape), -1, axis)


WIDE = False


def mx_kscale(k):
    if not WIDE:
        return np.ones(k)
    levels = np.array([10, -10, 5, -5, 0])
    if k % 512:
        return np.exp2(np.random.permutation(np.resize(levels, k // 32))).repeat(32)
    a = np.empty((k // 512, 16))
    for p in range(k // 512):
        a[p, :8] = np.random.permutation(np.resize(levels, 8))
        for g in range(8):
            far = levels[np.abs(levels - a[p, g]) >= 10]
            a[p, g + 8] = far[np.random.randint(len(far))]
    return np.exp2(a.ravel()).repeat(32)


BF16 = ml_dtypes.bfloat16


def bf(x):
    return np.asarray(x, np.float32).astype(BF16)


def f64(x):
    return np.asarray(x).astype(np.float64)


B, D, H, F, C, R = 128, 512, 16384, 256, 128, 32
EPS = 1e-12


def l2norm(x):
    n = np.sqrt((x ** 2).sum(-1, keepdims=True))
    return x / np.maximum(n, EPS)


def setup_inputs():
    s = mx_kscale(H)
    return {"features": bf(np.random.standard_normal((B, H)) * s),
            "ex_features": bf(np.random.standard_normal((D, H)) * s),
            "gW": bf(np.random.standard_normal((F, H)) / np.sqrt(H) / s[None, :]),
            "gb": bf(np.random.standard_normal(F) * 0.1)}


def reference(features, ex_features, gW, gb):
    wq = mxq(f64(gW), 1, "e4m3")
    f = (mxq(f64(features), 1, "e4m3") @ wq.T) + f64(gb)
    ex = (mxq(f64(ex_features), 1, "e4m3") @ wq.T) + f64(gb)
    return l2norm(f), l2norm(ex)

@@ -1,0 +1,227 @@
+from contextlib import ExitStack
+
+import concourse.masks as masks
+import concourse.mybir as mybir
+
+F32 = mybir.dt.float32
+BF16 = mybir.dt.bfloat16
+U32 = mybir.dt.uint32
+U8 = mybir.dt.uint8
+FP8X4 = mybir.dt.float8_e4m3fn_x4
+ACT = mybir.ActivationFunctionType
+ALU = mybir.AluOpType
+
+P = 128
+K = 16384
+F_OUT = 256
+EX_TILES = 4
+EPS = 1e-12
+
+PACK = 4
+K_PASS = PACK * P
+PASSES = K // K_PASS
+HALVES = 2
+SLOTS = 2
+CHUNK_PASSES = 4
+CHUNK_K = CHUNK_PASSES * K_PASS
+CHUNKS = K // CHUNK_K
+
+W_TILES = (0, 1)
+PHASE_ONE_X = (2, 3, 4)
+PHASE_TWO_X = (5, 6)
+PHASE_ONE_STEP = 2
+PHASE_TWO_STEP = 4
+ACC_BANKS = 3
+TRANSPOSE_BANKS = 8 - ACC_BANKS
+SETS_AHEAD = 4
+PIECES_AT_ENDS = CHUNK_PASSES // PHASE_ONE_STEP
+
+FLOPS = 2 * (1 + EX_TILES) * P * F_OUT * K
+
+
+def tile_minerva_detex_pa_k_kernel(tc, features, ex_features, gW, gb, out_0, out_1):
+    nc = tc.nc
+    rows_of = [gW[0:P, :], gW[P : 2 * P, :], features]
+    out_of = {2: out_0}
+    for i in range(EX_TILES):
+        out_of[len(rows_of)] = out_1[i * P : (i + 1) * P, :]
+        rows_of.append(ex_features[i * P : (i + 1) * P, :])
+
+    with ExitStack() as ctx:
+        ctx.enter_context(tc.manual_schedule())
+        consts = ctx.enter_context(tc.tile_pool(name="consts", bufs=1))
+        raws = ctx.enter_context(
+            tc.tile_pool(name="raws", bufs=(SETS_AHEAD + 1) * len(W_TILES + PHASE_ONE_X))
+        )
+        stage = ctx.enter_context(tc.tile_pool(name="stage", bufs=2 * TRANSPOSE_BANKS))
+        xq = ctx.enter_context(tc.tile_pool(name="xq", bufs=3 * PHASE_TWO_STEP))
+        tail = ctx.enter_context(tc.tile_pool(name="tail", bufs=len(PHASE_ONE_X)))
+        banks = ctx.enter_context(tc.psum_pool(name="banks", bufs=TRANSPOSE_BANKS))
+        accs = ctx.enter_context(tc.psum_pool(name="accs", bufs=ACC_BANKS))
+
+        load_sets = []
+        for c in range(CHUNKS):
+            at_an_end = c == 0 or c == CHUNKS - 1
+            load_sets.append((W_TILES + PHASE_ONE_X, c, PIECES_AT_ENDS if at_an_end else 1))
+        for c in range(CHUNKS):
+            load_sets.append((PHASE_TWO_X, c, 1))
+        raw = {}
+        sets_loaded = []
+
+        def load_next_set():
+            if len(sets_loaded) == len(load_sets):
+                return
+            row_tiles, c, pieces = load_sets[len(sets_loaded)]
+            sets_loaded.append(c)
+            for r in row_tiles:
+                raw[(r, c)] = raws.tile([P, CHUNK_K], BF16, name="chunk")
+            for piece in range(pieces):
+                cols = slice(piece * CHUNK_K // pieces, (piece + 1) * CHUNK_K // pieces)
+                for r in row_tiles:
+                    nc.sync.dma_start(
+                        out=raw[(r, c)][:, cols],
+                        in_=rows_of[r][:, c * CHUNK_K : (c + 1) * CHUNK_K][:, cols],
+                    )
+
+        for ahead in range(SETS_AHEAD):
+            load_next_set()
+
+        ident = consts.tile([P, P], F32, name="ident")
+        masks.make_identity(nc, ident[:])
+
+        bias_row = consts.tile([P, F_OUT], BF16, name="bias_row")
+        nc.vector.memset(bias_row[:], 0.0)
+        nc.scalar.dma_start(out=bias_row[0:1, :], in_=gb.rearrange("(o f) -> o f", o=1))
+        ones = consts.tile([P, P], BF16, name="ones")
+        nc.vector.memset(ones[:], 1.0)
+        bias = consts.tile([P, F_OUT], F32, name="bias")
+
+        def spread_bias():
+            bias_bank = accs.tile([P, F_OUT], F32, name="bias_bank", tag="acc")
+            nc.tensor.matmul(out=bias_bank[:], lhsT=ones[:], rhs=bias_row[:], start=True, stop=True)
+            nc.vector.tensor_copy(out=bias[:], in_=bias_bank[:])
+
+        one = consts.tile([P, 1], F32, name="one")
+        nc.vector.memset(one[:], 1.0)
+        one_root = consts.tile([P, 1], F32, name="one_root")
+        nc.scalar.sqrt(out=one_root[:], in_=one[:])
+
+        w_codes = consts.tile([P, PASSES, F_OUT], U32, name="w_codes", align_bytes=64)
+        w_scales = consts.tile([P, PASSES, F_OUT], U8, name="w_scales", align_bytes=64)
+        x_operand = {}
+        acc = {}
+
+        def transpose_and_quantise(x_tiles, with_w, first_pass, n_passes):
+            passes = range(first_pass, first_pass + n_passes)
+            if first_pass % CHUNK_PASSES == 0:
+                load_next_set()
+
+            units = []
+            if with_w:
+                for g in passes:
+                    units.append(([(r, g) for r in W_TILES], w_codes[:, g, :], w_scales[:, g, :]))
+            for r in x_tiles:
+                for g in passes[::SLOTS]:
+                    x_codes = xq.tile([P, SLOTS * P], U32, name="x_codes", align_bytes=64)
+                    x_scales = xq.tile([P, SLOTS * P], U8, name="x_scales", align_bytes=64)
+                    for a in range(SLOTS):
+                        cols = slice(a * P, (a + 1) * P)
+                        x_operand[(r, g + a)] = (x_codes[:, cols], x_scales[:, cols])
+                    units.append(([(r, g + a) for a in range(SLOTS)], x_codes[:], x_scales[:]))
+
+            def quantise(grouped, codes, scales):
+                nc.vector.quantize_mx(out=codes.bitcast(FP8X4), scales=scales, in_=grouped[:])
+
+            copied = None
+            for i, (slots, codes, scales) in enumerate(units):
+                bank = banks.tile([P, SLOTS, HALVES, P], F32, name="bank")
+                for a, (r, g) in enumerate(slots):
+                    words = raw[(r, g // CHUNK_PASSES)][:].bitcast(F32)
+                    for u in range(HALVES):
+                        first = (g % CHUNK_PASSES) * HALVES * P
+                        every_2nd = slice(first + u, first + HALVES * P, HALVES)
+                        nc.tensor.transpose(bank[:, a, u, :], words[:, every_2nd], ident[:])
+                grouped = stage.tile([P, SLOTS * P * PACK], BF16, name="grouped", align_bytes=64)
+                side_by_side = grouped[:].bitcast(F32).rearrange(
+                    "p (a r u) -> p a r u", a=SLOTS, u=HALVES
+                )
+                by_half = bank[:].rearrange("p a u r -> p a r u")
+                if i == 1:
+                    nc.vector.tensor_copy(out=side_by_side, in_=by_half)
+                else:
+                    nc.scalar.copy(out=side_by_side, in_=by_half)
+                if copied is not None:
+                    quantise(*copied)
+                copied = (grouped, codes, scales)
+            quantise(*copied)
+
+        def multiply(x_tiles, first_pass, n_passes):
+            for r in x_tiles:
+                for g in range(first_pass, first_pass + n_passes):
+                    if g == 0:
+                        acc[r] = accs.tile([P, F_OUT], F32, name="acc")
+                    codes, scales = x_operand[(r, g)]
+                    nc.tensor.matmul_mx(
+                        out=acc[r][:],
+                        lhsT=codes.bitcast(FP8X4),
+                        lhsT_scale=scales,
+                        rhs=w_codes[:, g, :].bitcast(FP8X4),
+                        rhs_scale=w_scales[:, g, :],
+                        start=(g == 0),
+                        stop=(g == PASSES - 1),
+                    )
+
+        y = {}
+        per_row = {}
+
+        def add_bias_and_square(x_tiles):
+            per_row["sum_sq"] = tail.tile([P, len(x_tiles)], F32, name="sum_sq")
+            for i, r in enumerate(x_tiles):
+                y[r] = tail.tile([P, F_OUT], F32, name="y")
+                nc.vector.tensor_tensor(out=y[r][:], in0=acc[r][:], in1=bias[:], op=ALU.add)
+                squares = tail.tile([P, F_OUT], F32, name="squares")
+                nc.scalar.activation(
+                    out=squares[:],
+                    in_=y[r][:],
+                    func=ACT.Square,
+                    accum_out=per_row["sum_sq"][:, i : i + 1],
+                )
+
+        def clamp_and_root(x_tiles):
+            clamped = tail.tile([P, len(x_tiles)], F32, name="clamped")
+            nc.vector.tensor_scalar_max(out=clamped[:], in0=per_row["sum_sq"][:], scalar1=EPS * EPS)
+            per_row["norm"] = tail.tile([P, len(x_tiles)], F32, name="norm")
+            nc.scalar.sqrt(out=per_row["norm"][:], in_=clamped[:])
+
+        def scale_and_store(x_tiles):
+            inverse = tail.tile([P, len(x_tiles)], F32, name="inverse")
+            nc.vector.reciprocal(out=inverse[:], in_=per_row["norm"][:])
+            for i, r in enumerate(x_tiles):
+                normalised = tail.tile([P, F_OUT], F32, name="normalised")
+                nc.vector.tensor_scalar_mul(out=normalised[:], in0=y[r][:], scalar1=inverse[:, i : i + 1])
+                nc.sync.dma_start(out=out_of[r], in_=normalised[:])
+
+        steps = []
+        for first_pass in range(0, PASSES, PHASE_ONE_STEP):
+            steps.append((PHASE_ONE_X, True, first_pass, PHASE_ONE_STEP))
+        phase_one_steps = len(steps)
+        for first_pass in range(0, PASSES, PHASE_TWO_STEP):
+            steps.append((PHASE_TWO_X, False, first_pass, PHASE_TWO_STEP))
+
+        transpose_and_quantise(*steps[0])
+        spread_bias()
+        for i in range(1, len(steps)):
+            transpose_and_quantise(*steps[i])
+            x_tiles, with_w, first_pass, n_passes = steps[i - 1]
+            multiply(x_tiles, first_pass, n_passes)
+            if i == phase_one_steps:
+                add_bias_and_square(PHASE_ONE_X)
+            if i == phase_one_steps + 1:
+                clamp_and_root(PHASE_ONE_X)
+            if i == phase_one_steps + 2:
+                scale_and_store(PHASE_ONE_X)
+        x_tiles, with_w, first_pass, n_passes = steps[-1]
+        multiply(x_tiles, first_pass, n_passes)
+        add_bias_and_square(PHASE_TWO_X)
+        clamp_and_root(PHASE_TWO_X)
+        scale_and_store(PHASE_TWO_X)

@@ -33,7 +33,8 @@ PHASE_ONE_STEP = 2
 PHASE_TWO_STEP = 4
 ACC_BANKS = 3
 TRANSPOSE_BANKS = 8 - ACC_BANKS
-SETS_AHEAD = 4
+RUN = 16
+SETS_AHEAD = 3
 PIECES_AT_ENDS = CHUNK_PASSES // PHASE_ONE_STEP
 
 FLOPS = 2 * (1 + EX_TILES) * P * F_OUT * K
@@ -52,6 +53,9 @@ def tile_minerva_detex_pa_k_kernel(tc, features, ex_features, gW, gb, out_0, out
         consts = ctx.enter_context(tc.tile_pool(name="consts", bufs=1))
         raws = ctx.enter_context(
             tc.tile_pool(name="raws", bufs=(SETS_AHEAD + 1) * len(W_TILES + PHASE_ONE_X))
+        )
+        regrouped = ctx.enter_context(
+            tc.tile_pool(name="regrouped", bufs=2 * len(W_TILES + PHASE_ONE_X) + 3)
         )
         stage = ctx.enter_context(tc.tile_pool(name="stage", bufs=2 * TRANSPOSE_BANKS))
         xq = ctx.enter_context(tc.tile_pool(name="xq", bufs=3 * PHASE_TWO_STEP))
@@ -111,7 +115,21 @@ def tile_minerva_detex_pa_k_kernel(tc, features, ex_features, gW, gb, out_0, out
         x_operand = {}
         acc = {}
 
-        def transpose_and_quantise(x_tiles, with_w, first_pass, n_passes):
+        halves = {}
+
+        def regroup(r, c, piece, pieces):
+            if piece == 0:
+                halves[(r, c)] = regrouped.tile([P, HALVES, CHUNK_K // HALVES], BF16, name="halves")
+            n = CHUNK_K // pieces
+            source = raw[(r, c)][:, piece * n : (piece + 1) * n]
+            nc.vector.tensor_copy(
+                out=halves[(r, c)][:, :, piece * n // HALVES : (piece + 1) * n // HALVES].rearrange(
+                    "p u (q e) -> p u q e", e=RUN
+                ),
+                in_=source.rearrange("p (q u e) -> p u q e", u=HALVES, e=RUN),
+            )
+
+        def transpose_and_quantise(x_tiles, with_w, first_pass, n_passes, jobs):
             passes = range(first_pass, first_pass + n_passes)
             if first_pass % CHUNK_PASSES == 0:
                 load_next_set()
@@ -136,20 +154,18 @@ def tile_minerva_detex_pa_k_kernel(tc, features, ex_features, gW, gb, out_0, out
             for i, (slots, codes, scales) in enumerate(units):
                 bank = banks.tile([P, SLOTS, HALVES, P], F32, name="bank")
                 for a, (r, g) in enumerate(slots):
-                    words = raw[(r, g // CHUNK_PASSES)][:].bitcast(F32)
                     for u in range(HALVES):
-                        first = (g % CHUNK_PASSES) * HALVES * P
-                        every_2nd = slice(first + u, first + HALVES * P, HALVES)
-                        nc.tensor.transpose(bank[:, a, u, :], words[:, every_2nd], ident[:])
+                        words = halves[(r, g // CHUNK_PASSES)][:, u, :].bitcast(F32)
+                        first = (g % CHUNK_PASSES) * P
+                        nc.tensor.transpose(bank[:, a, u, :], words[:, first : first + P], ident[:])
                 grouped = stage.tile([P, SLOTS * P * PACK], BF16, name="grouped", align_bytes=64)
                 side_by_side = grouped[:].bitcast(F32).rearrange(
                     "p (a r u) -> p a r u", a=SLOTS, u=HALVES
                 )
                 by_half = bank[:].rearrange("p a u r -> p a r u")
-                if i == 1:
-                    nc.vector.tensor_copy(out=side_by_side, in_=by_half)
-                else:
-                    nc.scalar.copy(out=side_by_side, in_=by_half)
+                nc.scalar.copy(out=side_by_side, in_=by_half)
+                for job in jobs[i * len(jobs) // len(units) : (i + 1) * len(jobs) // len(units)]:
+                    regroup(*job)
                 if copied is not None:
                     quantise(*copied)
                 copied = (grouped, codes, scales)
@@ -208,10 +224,24 @@ def tile_minerva_detex_pa_k_kernel(tc, features, ex_features, gW, gb, out_0, out
         for first_pass in range(0, PASSES, PHASE_TWO_STEP):
             steps.append((PHASE_TWO_X, False, first_pass, PHASE_TWO_STEP))
 
-        transpose_and_quantise(*steps[0])
+        set_jobs = []
+        for row_tiles, c, pieces in load_sets:
+            set_jobs.append([(r, c, piece, pieces) for piece in range(pieces) for r in row_tiles])
+        step_jobs = []
+        for n, (row_tiles, c, pieces) in enumerate(load_sets):
+            n_steps = PIECES_AT_ENDS if len(row_tiles) == len(W_TILES + PHASE_ONE_X) else 1
+            ahead = set_jobs[n + 1] if n + 1 < len(load_sets) else []
+            for k in range(n_steps):
+                step_jobs.append(ahead[k * len(ahead) // n_steps : (k + 1) * len(ahead) // n_steps])
+        n_first = len(W_TILES + PHASE_ONE_X)
+        for job in set_jobs[0][:n_first]:
+            regroup(*job)
+        step_jobs[0] = set_jobs[0][n_first:] + step_jobs[0]
+
+        transpose_and_quantise(*steps[0], step_jobs[0])
         spread_bias()
         for i in range(1, len(steps)):
-            transpose_and_quantise(*steps[i])
+            transpose_and_quantise(*steps[i], step_jobs[i])
             x_tiles, with_w, first_pass, n_passes = steps[i - 1]
             multiply(x_tiles, first_pass, n_passes)
             if i == phase_one_steps:

@@ -34,7 +34,9 @@ PHASE_TWO_STEP = 4
 ACC_BANKS = 3
 TRANSPOSE_BANKS = 8 - ACC_BANKS
 RUN = 16
-SETS_AHEAD = 3
+PAIR = 2
+PAIR_K = PAIR * K_PASS
+SETS_AHEAD = 4
 PIECES_AT_ENDS = CHUNK_PASSES // PHASE_ONE_STEP
 
 FLOPS = 2 * (1 + EX_TILES) * P * F_OUT * K
@@ -115,19 +117,32 @@ def tile_minerva_detex_pa_k_kernel(tc, features, ex_features, gW, gb, out_0, out
         x_operand = {}
         acc = {}
 
-        halves = {}
+        odds = {}
 
-        def regroup(r, c, piece, pieces):
+        def split(view, pairs):
+            return view.rearrange("p (j w i h e) -> p j w i h e", j=pairs, w=2, h=2, e=RUN)
+
+        def take_odds(r, c, piece, pieces):
             if piece == 0:
-                halves[(r, c)] = regrouped.tile([P, HALVES, CHUNK_K // HALVES], BF16, name="halves")
+                odds[(r, c)] = regrouped.tile([P, CHUNK_K // HALVES], BF16, name="odd_halves")
             n = CHUNK_K // pieces
             source = raw[(r, c)][:, piece * n : (piece + 1) * n]
+            target = odds[(r, c)][:, piece * n // HALVES : (piece + 1) * n // HALVES]
             nc.vector.tensor_copy(
-                out=halves[(r, c)][:, :, piece * n // HALVES : (piece + 1) * n // HALVES].rearrange(
-                    "p u (q e) -> p u q e", e=RUN
-                ),
-                in_=source.rearrange("p (q u e) -> p u q e", u=HALVES, e=RUN),
+                out=target.rearrange("p (j i w e) -> p j w i e", j=n // PAIR_K, w=2, e=RUN),
+                in_=split(source, n // PAIR_K)[:, :, :, :, 1, :],
             )
+
+        def move_evens(r, c, piece, pieces):
+            n = CHUNK_K // pieces
+            halves = split(raw[(r, c)][:, piece * n : (piece + 1) * n], n // PAIR_K)
+            nc.vector.tensor_copy(out=halves[:, :, 0, :, 1, :], in_=halves[:, :, 1, :, 0, :])
+
+        def regroup(kind, *job):
+            if kind == "odds":
+                take_odds(*job)
+            else:
+                move_evens(*job)
 
         def transpose_and_quantise(x_tiles, with_w, first_pass, n_passes, jobs):
             passes = range(first_pass, first_pass + n_passes)
@@ -154,9 +169,12 @@ def tile_minerva_detex_pa_k_kernel(tc, features, ex_features, gW, gb, out_0, out
             for i, (slots, codes, scales) in enumerate(units):
                 bank = banks.tile([P, SLOTS, HALVES, P], F32, name="bank")
                 for a, (r, g) in enumerate(slots):
-                    for u in range(HALVES):
-                        words = halves[(r, g // CHUNK_PASSES)][:, u, :].bitcast(F32)
-                        first = (g % CHUNK_PASSES) * P
+                    chunk = (r, g // CHUNK_PASSES)
+                    pair, m = divmod(g % CHUNK_PASSES, PAIR)
+                    for u, (tile, first) in enumerate(
+                        ((raw[chunk], (2 * PAIR * pair + m) * P), (odds[chunk], (pair * PAIR + m) * P))
+                    ):
+                        words = tile[:].bitcast(F32)
                         nc.tensor.transpose(bank[:, a, u, :], words[:, first : first + P], ident[:])
                 grouped = stage.tile([P, SLOTS * P * PACK], BF16, name="grouped", align_bytes=64)
                 side_by_side = grouped[:].bitcast(F32).rearrange(
@@ -226,14 +244,21 @@ def tile_minerva_detex_pa_k_kernel(tc, features, ex_features, gW, gb, out_0, out
 
         set_jobs = []
         for row_tiles, c, pieces in load_sets:
-            set_jobs.append([(r, c, piece, pieces) for piece in range(pieces) for r in row_tiles])
+            jobs = []
+            for piece in range(pieces):
+                for i, r in enumerate(row_tiles):
+                    jobs.append(("odds", r, c, piece, pieces))
+                    if i > 0:
+                        jobs.append(("evens", row_tiles[i - 1], c, piece, pieces))
+                jobs.append(("evens", row_tiles[-1], c, piece, pieces))
+            set_jobs.append(jobs)
         step_jobs = []
         for n, (row_tiles, c, pieces) in enumerate(load_sets):
             n_steps = PIECES_AT_ENDS if len(row_tiles) == len(W_TILES + PHASE_ONE_X) else 1
             ahead = set_jobs[n + 1] if n + 1 < len(load_sets) else []
             for k in range(n_steps):
                 step_jobs.append(ahead[k * len(ahead) // n_steps : (k + 1) * len(ahead) // n_steps])
-        n_first = len(W_TILES + PHASE_ONE_X)
+        n_first = 2 * len(W_TILES + PHASE_ONE_X)
         for job in set_jobs[0][:n_first]:
             regroup(*job)
         step_jobs[0] = set_jobs[0][n_first:] + step_jobs[0]

@@ -25,19 +25,18 @@ SLOTS = 2
 CHUNK_PASSES = 4
 CHUNK_K = CHUNK_PASSES * K_PASS
 CHUNKS = K // CHUNK_K
-
-W_TILES = (0, 1)
-PHASE_ONE_X = (2, 3, 4)
-PHASE_TWO_X = (5, 6)
-PHASE_ONE_STEP = 2
-PHASE_TWO_STEP = 4
-ACC_BANKS = 3
-TRANSPOSE_BANKS = 8 - ACC_BANKS
 RUN = 16
 PAIR = 2
 PAIR_K = PAIR * K_PASS
-SETS_AHEAD = 4
-PIECES_AT_ENDS = CHUNK_PASSES // PHASE_ONE_STEP
+
+W_TILES = (0, 1)
+X_TILES = (2, 3, 4, 5, 6)
+ACC_BANKS = 3
+TRANSPOSE_BANKS = 8 - ACC_BANKS
+CHUNKS_AHEAD = 14
+REGROUP_AHEAD = 8
+MULTIPLY_EVERY = 6
+MULTIPLY_BEHIND = 9
 
 FLOPS = 2 * (1 + EX_TILES) * P * F_OUT * K
 
@@ -53,44 +52,28 @@ def tile_minerva_detex_pa_k_kernel(tc, features, ex_features, gW, gb, out_0, out
     with ExitStack() as ctx:
         ctx.enter_context(tc.manual_schedule())
         consts = ctx.enter_context(tc.tile_pool(name="consts", bufs=1))
-        raws = ctx.enter_context(
-            tc.tile_pool(name="raws", bufs=(SETS_AHEAD + 1) * len(W_TILES + PHASE_ONE_X))
-        )
-        regrouped = ctx.enter_context(
-            tc.tile_pool(name="regrouped", bufs=2 * len(W_TILES + PHASE_ONE_X) + 3)
-        )
-        stage = ctx.enter_context(tc.tile_pool(name="stage", bufs=2 * TRANSPOSE_BANKS))
-        xq = ctx.enter_context(tc.tile_pool(name="xq", bufs=3 * PHASE_TWO_STEP))
-        tail = ctx.enter_context(tc.tile_pool(name="tail", bufs=len(PHASE_ONE_X)))
+        raws = ctx.enter_context(tc.tile_pool(name="raws", bufs=24))
+        regrouped = ctx.enter_context(tc.tile_pool(name="regrouped", bufs=12))
+        stage = ctx.enter_context(tc.tile_pool(name="stage", bufs=8))
+        xq = ctx.enter_context(tc.tile_pool(name="xq", bufs=14))
+        tail = ctx.enter_context(tc.tile_pool(name="tail", bufs=len(X_TILES)))
         banks = ctx.enter_context(tc.psum_pool(name="banks", bufs=TRANSPOSE_BANKS))
         accs = ctx.enter_context(tc.psum_pool(name="accs", bufs=ACC_BANKS))
 
-        load_sets = []
-        for c in range(CHUNKS):
-            at_an_end = c == 0 or c == CHUNKS - 1
-            load_sets.append((W_TILES + PHASE_ONE_X, c, PIECES_AT_ENDS if at_an_end else 1))
-        for c in range(CHUNKS):
-            load_sets.append((PHASE_TWO_X, c, 1))
+        loads = [(r, c) for c in range(CHUNKS) for r in W_TILES + X_TILES]
+        load_index = {}
         raw = {}
-        sets_loaded = []
 
-        def load_next_set():
-            if len(sets_loaded) == len(load_sets):
-                return
-            row_tiles, c, pieces = load_sets[len(sets_loaded)]
-            sets_loaded.append(c)
-            for r in row_tiles:
-                raw[(r, c)] = raws.tile([P, CHUNK_K], BF16, name="chunk")
-            for piece in range(pieces):
-                cols = slice(piece * CHUNK_K // pieces, (piece + 1) * CHUNK_K // pieces)
-                for r in row_tiles:
-                    nc.sync.dma_start(
-                        out=raw[(r, c)][:, cols],
-                        in_=rows_of[r][:, c * CHUNK_K : (c + 1) * CHUNK_K][:, cols],
-                    )
+        def load_next():
+            r, c = loads[len(raw)]
+            load_index[(r, c)] = len(raw)
+            raw[(r, c)] = raws.tile([P, CHUNK_K], BF16, name="chunk")
+            nc.sync.dma_start(
+                out=raw[(r, c)][:], in_=rows_of[r][:, c * CHUNK_K : (c + 1) * CHUNK_K]
+            )
 
-        for ahead in range(SETS_AHEAD):
-            load_next_set()
+        for ahead in range(CHUNKS_AHEAD):
+            load_next()
 
         ident = consts.tile([P, P], F32, name="ident")
         masks.make_identity(nc, ident[:])
@@ -101,182 +84,155 @@ def tile_minerva_detex_pa_k_kernel(tc, features, ex_features, gW, gb, out_0, out
         ones = consts.tile([P, P], BF16, name="ones")
         nc.vector.memset(ones[:], 1.0)
         bias = consts.tile([P, F_OUT], F32, name="bias")
-
-        def spread_bias():
-            bias_bank = accs.tile([P, F_OUT], F32, name="bias_bank", tag="acc")
-            nc.tensor.matmul(out=bias_bank[:], lhsT=ones[:], rhs=bias_row[:], start=True, stop=True)
-            nc.vector.tensor_copy(out=bias[:], in_=bias_bank[:])
+        bias_bank = banks.tile([P, F_OUT], F32, name="bias_bank", tag="bank")
+        nc.tensor.matmul(out=bias_bank[:], lhsT=ones[:], rhs=bias_row[:], start=True, stop=True)
+        nc.vector.tensor_copy(out=bias[:], in_=bias_bank[:])
 
         one = consts.tile([P, 1], F32, name="one")
         nc.vector.memset(one[:], 1.0)
         one_root = consts.tile([P, 1], F32, name="one_root")
-        nc.scalar.sqrt(out=one_root[:], in_=one[:])
-
-        w_codes = consts.tile([P, PASSES, F_OUT], U32, name="w_codes", align_bytes=64)
-        w_scales = consts.tile([P, PASSES, F_OUT], U8, name="w_scales", align_bytes=64)
-        x_operand = {}
-        acc = {}
+        nc.scalar.activation(out=one_root[:], in_=one[:], func=ACT.Abs_reciprocal_sqrt)
 
         odds = {}
 
         def split(view, pairs):
             return view.rearrange("p (j w i h e) -> p j w i h e", j=pairs, w=2, h=2, e=RUN)
 
-        def take_odds(r, c, piece, pieces):
-            if piece == 0:
-                odds[(r, c)] = regrouped.tile([P, CHUNK_K // HALVES], BF16, name="odd_halves")
-            n = CHUNK_K // pieces
-            source = raw[(r, c)][:, piece * n : (piece + 1) * n]
-            target = odds[(r, c)][:, piece * n // HALVES : (piece + 1) * n // HALVES]
+        def take_odds(r, c):
+            odds[(r, c)] = regrouped.tile([P, CHUNK_K // HALVES], BF16, name="odd_halves")
+            pairs = CHUNK_PASSES // PAIR
             nc.vector.tensor_copy(
-                out=target.rearrange("p (j i w e) -> p j w i e", j=n // PAIR_K, w=2, e=RUN),
-                in_=split(source, n // PAIR_K)[:, :, :, :, 1, :],
+                out=odds[(r, c)][:].rearrange("p (j i w e) -> p j w i e", j=pairs, w=2, e=RUN),
+                in_=split(raw[(r, c)][:], pairs)[:, :, :, :, 1, :],
             )
 
-        def move_evens(r, c, piece, pieces):
-            n = CHUNK_K // pieces
-            halves = split(raw[(r, c)][:, piece * n : (piece + 1) * n], n // PAIR_K)
+        def move_evens(r, c):
+            halves = split(raw[(r, c)][:], CHUNK_PASSES // PAIR)
             nc.vector.tensor_copy(out=halves[:, :, 0, :, 1, :], in_=halves[:, :, 1, :, 0, :])
 
-        def regroup(kind, *job):
-            if kind == "odds":
-                take_odds(*job)
-            else:
-                move_evens(*job)
-
-        def transpose_and_quantise(x_tiles, with_w, first_pass, n_passes, jobs):
-            passes = range(first_pass, first_pass + n_passes)
-            if first_pass % CHUNK_PASSES == 0:
-                load_next_set()
-
-            units = []
-            if with_w:
-                for g in passes:
-                    units.append(([(r, g) for r in W_TILES], w_codes[:, g, :], w_scales[:, g, :]))
-            for r in x_tiles:
+        w_codes = consts.tile([P, PASSES, F_OUT], U32, name="w_codes", align_bytes=64)
+        w_scales = consts.tile([P, PASSES, F_OUT], U8, name="w_scales", align_bytes=64)
+        units = []
+        for c in range(CHUNKS):
+            passes = range(c * CHUNK_PASSES, (c + 1) * CHUNK_PASSES)
+            for g in passes:
+                units.append([(r, g) for r in W_TILES])
+            for r in X_TILES:
                 for g in passes[::SLOTS]:
-                    x_codes = xq.tile([P, SLOTS * P], U32, name="x_codes", align_bytes=64)
-                    x_scales = xq.tile([P, SLOTS * P], U8, name="x_scales", align_bytes=64)
-                    for a in range(SLOTS):
-                        cols = slice(a * P, (a + 1) * P)
-                        x_operand[(r, g + a)] = (x_codes[:, cols], x_scales[:, cols])
-                    units.append(([(r, g + a) for a in range(SLOTS)], x_codes[:], x_scales[:]))
+                    units.append([(r, g + a) for a in range(SLOTS)])
+        jobs = []
+        wanted = set()
+        for n, slots in enumerate(units):
+            for r, g in slots:
+                if (r, g // CHUNK_PASSES) not in wanted:
+                    wanted.add((r, g // CHUNK_PASSES))
+                    jobs.append((n, r, g // CHUNK_PASSES))
 
-            def quantise(grouped, codes, scales):
-                nc.vector.quantize_mx(out=codes.bitcast(FP8X4), scales=scales, in_=grouped[:])
+        def transpose(slots):
+            bank = banks.tile([P, SLOTS, HALVES, P], F32, name="bank")
+            for a, (r, g) in enumerate(slots):
+                chunk = (r, g // CHUNK_PASSES)
+                pair, m = divmod(g % CHUNK_PASSES, PAIR)
+                evens = raw[chunk][:].bitcast(F32)
+                first = (HALVES * PAIR * pair + m) * P
+                nc.tensor.transpose(bank[:, a, 0, :], evens[:, first : first + P], ident[:])
+                words = odds[chunk][:].bitcast(F32)
+                first = (PAIR * pair + m) * P
+                nc.tensor.transpose(bank[:, a, 1, :], words[:, first : first + P], ident[:])
+            return bank
 
-            copied = None
-            for i, (slots, codes, scales) in enumerate(units):
-                bank = banks.tile([P, SLOTS, HALVES, P], F32, name="bank")
-                for a, (r, g) in enumerate(slots):
-                    chunk = (r, g // CHUNK_PASSES)
-                    pair, m = divmod(g % CHUNK_PASSES, PAIR)
-                    for u, (tile, first) in enumerate(
-                        ((raw[chunk], (2 * PAIR * pair + m) * P), (odds[chunk], (pair * PAIR + m) * P))
-                    ):
-                        words = tile[:].bitcast(F32)
-                        nc.tensor.transpose(bank[:, a, u, :], words[:, first : first + P], ident[:])
-                grouped = stage.tile([P, SLOTS * P * PACK], BF16, name="grouped", align_bytes=64)
-                side_by_side = grouped[:].bitcast(F32).rearrange(
-                    "p (a r u) -> p a r u", a=SLOTS, u=HALVES
+        def interleave(bank):
+            grouped = stage.tile([P, SLOTS * P * PACK], BF16, name="grouped", align_bytes=64)
+            nc.scalar.copy(
+                out=grouped[:].bitcast(F32).rearrange("p (a r u) -> p a r u", a=SLOTS, u=HALVES),
+                in_=bank[:].rearrange("p a u r -> p a r u"),
+            )
+            return grouped
+
+        products = []
+
+        def operand(n, slots):
+            if slots[0][0] in W_TILES:
+                g = slots[0][1]
+                return w_codes[:, g, :], w_scales[:, g, :]
+            codes = xq.tile([P, SLOTS * P], U32, name="x_codes", align_bytes=64)
+            scales = xq.tile([P, SLOTS * P], U8, name="x_scales", align_bytes=64)
+            for a, (r, g) in enumerate(slots):
+                cols = slice(a * P, (a + 1) * P)
+                products.append((n, r, g, codes[:, cols], scales[:, cols]))
+            return codes[:], scales[:]
+
+        def quantise(grouped, codes, scales):
+            nc.vector.quantize_mx(out=codes.bitcast(FP8X4), scales=scales, in_=grouped[:])
+
+        acc_bank = [accs.tile([P, 2, F_OUT], F32, name="acc") for b in range(ACC_BANKS)]
+        acc = {r: acc_bank[i // 2][:, i % 2, :] for i, r in enumerate(X_TILES)}
+        opens = X_TILES[0::2]
+        closes = X_TILES[1::2] + X_TILES[-1:]
+
+        issued = []
+
+        def multiply(up_to):
+            while len(issued) < len(products) and products[len(issued)][0] <= up_to:
+                n, r, g, codes, scales = products[len(issued)]
+                issued.append(n)
+                nc.tensor.matmul_mx(
+                    out=acc[r],
+                    lhsT=codes.bitcast(FP8X4),
+                    lhsT_scale=scales,
+                    rhs=w_codes[:, g, :].bitcast(FP8X4),
+                    rhs_scale=w_scales[:, g, :],
+                    start=(g == 0 and r in opens),
+                    stop=(g == PASSES - 1 and r in closes),
                 )
-                by_half = bank[:].rearrange("p a u r -> p a r u")
-                nc.scalar.copy(out=side_by_side, in_=by_half)
-                for job in jobs[i * len(jobs) // len(units) : (i + 1) * len(jobs) // len(units)]:
-                    regroup(*job)
-                if copied is not None:
-                    quantise(*copied)
-                copied = (grouped, codes, scales)
-            quantise(*copied)
 
-        def multiply(x_tiles, first_pass, n_passes):
-            for r in x_tiles:
-                for g in range(first_pass, first_pass + n_passes):
-                    if g == 0:
-                        acc[r] = accs.tile([P, F_OUT], F32, name="acc")
-                    codes, scales = x_operand[(r, g)]
-                    nc.tensor.matmul_mx(
-                        out=acc[r][:],
-                        lhsT=codes.bitcast(FP8X4),
-                        lhsT_scale=scales,
-                        rhs=w_codes[:, g, :].bitcast(FP8X4),
-                        rhs_scale=w_scales[:, g, :],
-                        start=(g == 0),
-                        stop=(g == PASSES - 1),
-                    )
+        done = 0
+        copied = None
+        for n, slots in enumerate(units):
+            while len(raw) < min(len(loads), load_index[(slots[0][0], slots[0][1] // CHUNK_PASSES)] + CHUNKS_AHEAD):
+                load_next()
+            while done < len(jobs) and jobs[done][0] <= n:
+                take_odds(*jobs[done][1:])
+                move_evens(*jobs[done][1:])
+                done += 1
+            grouped = interleave(transpose(slots))
+            begun = done < len(jobs) and jobs[done][0] <= n + REGROUP_AHEAD
+            if begun:
+                take_odds(*jobs[done][1:])
+            if copied is not None:
+                quantise(*copied)
+            if begun:
+                move_evens(*jobs[done][1:])
+                done += 1
+            codes, scales = operand(n, slots)
+            copied = (grouped, codes, scales)
+            if n % MULTIPLY_EVERY == MULTIPLY_EVERY - 1:
+                multiply(n - MULTIPLY_BEHIND)
+        quantise(*copied)
+        multiply(len(units))
 
         y = {}
-        per_row = {}
-
-        def add_bias_and_square(x_tiles):
-            per_row["sum_sq"] = tail.tile([P, len(x_tiles)], F32, name="sum_sq")
-            for i, r in enumerate(x_tiles):
+        groups = [X_TILES[:-1], X_TILES[-1:]]
+        group_sums = [tail.tile([P, len(group)], F32, name="sum_sq") for group in groups]
+        for group, sum_sq in zip(groups, group_sums):
+            for i, r in enumerate(group):
                 y[r] = tail.tile([P, F_OUT], F32, name="y")
-                nc.vector.tensor_tensor(out=y[r][:], in0=acc[r][:], in1=bias[:], op=ALU.add)
+                nc.vector.tensor_tensor(out=y[r][:], in0=acc[r], in1=bias[:], op=ALU.add)
                 squares = tail.tile([P, F_OUT], F32, name="squares")
                 nc.scalar.activation(
-                    out=squares[:],
-                    in_=y[r][:],
-                    func=ACT.Square,
-                    accum_out=per_row["sum_sq"][:, i : i + 1],
+                    out=squares[:], in_=y[r][:], func=ACT.Square, accum_out=sum_sq[:, i : i + 1]
                 )
-
-        def clamp_and_root(x_tiles):
-            clamped = tail.tile([P, len(x_tiles)], F32, name="clamped")
-            nc.vector.tensor_scalar_max(out=clamped[:], in0=per_row["sum_sq"][:], scalar1=EPS * EPS)
-            per_row["norm"] = tail.tile([P, len(x_tiles)], F32, name="norm")
-            nc.scalar.sqrt(out=per_row["norm"][:], in_=clamped[:])
-
-        def scale_and_store(x_tiles):
-            inverse = tail.tile([P, len(x_tiles)], F32, name="inverse")
-            nc.vector.reciprocal(out=inverse[:], in_=per_row["norm"][:])
-            for i, r in enumerate(x_tiles):
+        inverses = []
+        for group, sum_sq in zip(groups, group_sums):
+            clamped = tail.tile([P, len(group)], F32, name="clamped")
+            nc.vector.tensor_scalar_max(out=clamped[:], in0=sum_sq[:], scalar1=EPS * EPS)
+            inverse = tail.tile([P, len(group)], F32, name="inverse")
+            nc.scalar.activation(out=inverse[:], in_=clamped[:], func=ACT.Abs_reciprocal_sqrt)
+            inverses.append(inverse)
+        for group, inverse in zip(groups, inverses):
+            for i, r in enumerate(group):
                 normalised = tail.tile([P, F_OUT], F32, name="normalised")
-                nc.vector.tensor_scalar_mul(out=normalised[:], in0=y[r][:], scalar1=inverse[:, i : i + 1])
+                nc.vector.tensor_scalar_mul(
+                    out=normalised[:], in0=y[r][:], scalar1=inverse[:, i : i + 1]
+                )
                 nc.sync.dma_start(out=out_of[r], in_=normalised[:])
-
-        steps = []
-        for first_pass in range(0, PASSES, PHASE_ONE_STEP):
-            steps.append((PHASE_ONE_X, True, first_pass, PHASE_ONE_STEP))
-        phase_one_steps = len(steps)
-        for first_pass in range(0, PASSES, PHASE_TWO_STEP):
-            steps.append((PHASE_TWO_X, False, first_pass, PHASE_TWO_STEP))
-
-        set_jobs = []
-        for row_tiles, c, pieces in load_sets:
-            jobs = []
-            for piece in range(pieces):
-                for i, r in enumerate(row_tiles):
-                    jobs.append(("odds", r, c, piece, pieces))
-                    if i > 0:
-                        jobs.append(("evens", row_tiles[i - 1], c, piece, pieces))
-                jobs.append(("evens", row_tiles[-1], c, piece, pieces))
-            set_jobs.append(jobs)
-        step_jobs = []
-        for n, (row_tiles, c, pieces) in enumerate(load_sets):
-            n_steps = PIECES_AT_ENDS if len(row_tiles) == len(W_TILES + PHASE_ONE_X) else 1
-            ahead = set_jobs[n + 1] if n + 1 < len(load_sets) else []
-            for k in range(n_steps):
-                step_jobs.append(ahead[k * len(ahead) // n_steps : (k + 1) * len(ahead) // n_steps])
-        n_first = 2 * len(W_TILES + PHASE_ONE_X)
-        for job in set_jobs[0][:n_first]:
-            regroup(*job)
-        step_jobs[0] = set_jobs[0][n_first:] + step_jobs[0]
-
-        transpose_and_quantise(*steps[0], step_jobs[0])
-        spread_bias()
-        for i in range(1, len(steps)):
-            transpose_and_quantise(*steps[i], step_jobs[i])
-            x_tiles, with_w, first_pass, n_passes = steps[i - 1]
-            multiply(x_tiles, first_pass, n_passes)
-            if i == phase_one_steps:
-                add_bias_and_square(PHASE_ONE_X)
-            if i == phase_one_steps + 1:
-                clamp_and_root(PHASE_ONE_X)
-            if i == phase_one_steps + 2:
-                scale_and_store(PHASE_ONE_X)
-        x_tiles, with_w, first_pass, n_passes = steps[-1]
-        multiply(x_tiles, first_pass, n_passes)
-        add_bias_and_square(PHASE_TWO_X)
-        clamp_and_root(PHASE_TWO_X)
-        scale_and_store(PHASE_TWO_X)

@@ -84,9 +84,11 @@ def tile_minerva_detex_pa_k_kernel(tc, features, ex_features, gW, gb, out_0, out
         ones = consts.tile([P, P], BF16, name="ones")
         nc.vector.memset(ones[:], 1.0)
         bias = consts.tile([P, F_OUT], F32, name="bias")
-        bias_bank = banks.tile([P, F_OUT], F32, name="bias_bank", tag="bank")
-        nc.tensor.matmul(out=bias_bank[:], lhsT=ones[:], rhs=bias_row[:], start=True, stop=True)
-        nc.vector.tensor_copy(out=bias[:], in_=bias_bank[:])
+
+        def spread_bias():
+            bias_bank = banks.tile([P, F_OUT], F32, name="bias_bank", tag="bank")
+            nc.tensor.matmul(out=bias_bank[:], lhsT=ones[:], rhs=bias_row[:], start=True, stop=True)
+            nc.vector.tensor_copy(out=bias[:], in_=bias_bank[:])
 
         one = consts.tile([P, 1], F32, name="one")
         nc.vector.memset(one[:], 1.0)
@@ -208,6 +210,8 @@ def tile_minerva_detex_pa_k_kernel(tc, features, ex_features, gW, gb, out_0, out
             copied = (grouped, codes, scales)
             if n % MULTIPLY_EVERY == MULTIPLY_EVERY - 1:
                 multiply(n - MULTIPLY_BEHIND)
+            if n == MULTIPLY_BEHIND:
+                spread_bias()
         quantise(*copied)
         multiply(len(units))
 

@@ -22,9 +22,8 @@ K_PASS = PACK * P
 PASSES = K // K_PASS
 HALVES = 2
 SLOTS = 2
-CHUNK_PASSES = 4
-CHUNK_K = CHUNK_PASSES * K_PASS
-CHUNKS = K // CHUNK_K
+SET_PASSES = (2, 6, 8, 8, 4, 4)
+LONGEST = max(SET_PASSES)
 RUN = 16
 PAIR = 2
 PAIR_K = PAIR * K_PASS
@@ -33,10 +32,12 @@ W_TILES = (0, 1)
 X_TILES = (2, 3, 4, 5, 6)
 ACC_BANKS = 3
 TRANSPOSE_BANKS = 8 - ACC_BANKS
-CHUNKS_AHEAD = 14
-REGROUP_AHEAD = 8
+CHUNKS_AHEAD = 8
+REGROUP_AHEAD = 10
+REGROUP_PASSES = 4
 MULTIPLY_EVERY = 6
 MULTIPLY_BEHIND = 9
+MULTIPLY_RUN = 9
 
 FLOPS = 2 * (1 + EX_TILES) * P * F_OUT * K
 
@@ -52,24 +53,31 @@ def tile_minerva_detex_pa_k_kernel(tc, features, ex_features, gW, gb, out_0, out
     with ExitStack() as ctx:
         ctx.enter_context(tc.manual_schedule())
         consts = ctx.enter_context(tc.tile_pool(name="consts", bufs=1))
-        raws = ctx.enter_context(tc.tile_pool(name="raws", bufs=24))
-        regrouped = ctx.enter_context(tc.tile_pool(name="regrouped", bufs=12))
+        raws = ctx.enter_context(tc.tile_pool(name="raws", bufs=12))
+        regrouped = ctx.enter_context(tc.tile_pool(name="regrouped", bufs=14))
         stage = ctx.enter_context(tc.tile_pool(name="stage", bufs=8))
-        xq = ctx.enter_context(tc.tile_pool(name="xq", bufs=14))
+        xq = ctx.enter_context(tc.tile_pool(name="xq", bufs=24))
         tail = ctx.enter_context(tc.tile_pool(name="tail", bufs=len(X_TILES)))
+        thrown = ctx.enter_context(tc.tile_pool(name="thrown", bufs=2))
         banks = ctx.enter_context(tc.psum_pool(name="banks", bufs=TRANSPOSE_BANKS))
         accs = ctx.enter_context(tc.psum_pool(name="accs", bufs=ACC_BANKS))
 
-        loads = [(r, c) for c in range(CHUNKS) for r in W_TILES + X_TILES]
+        first_pass = [sum(SET_PASSES[:c]) for c in range(len(SET_PASSES))]
+        set_of = {}
+        for c, n in enumerate(SET_PASSES):
+            for g in range(first_pass[c], first_pass[c] + n):
+                set_of[g] = c
+        loads = [(r, c) for c in range(len(SET_PASSES)) for r in W_TILES + X_TILES]
         load_index = {}
         raw = {}
 
         def load_next():
             r, c = loads[len(raw)]
             load_index[(r, c)] = len(raw)
-            raw[(r, c)] = raws.tile([P, CHUNK_K], BF16, name="chunk")
+            raw[(r, c)] = raws.tile([P, LONGEST * K_PASS], BF16, name="chunk")
+            k = slice(first_pass[c] * K_PASS, (first_pass[c] + SET_PASSES[c]) * K_PASS)
             nc.sync.dma_start(
-                out=raw[(r, c)][:], in_=rows_of[r][:, c * CHUNK_K : (c + 1) * CHUNK_K]
+                out=raw[(r, c)][:, : SET_PASSES[c] * K_PASS], in_=rows_of[r][:, k]
             )
 
         for ahead in range(CHUNKS_AHEAD):
@@ -96,50 +104,58 @@ def tile_minerva_detex_pa_k_kernel(tc, features, ex_features, gW, gb, out_0, out
         nc.scalar.activation(out=one_root[:], in_=one[:], func=ACT.Abs_reciprocal_sqrt)
 
         odds = {}
+        job_of = {}
 
         def split(view, pairs):
             return view.rearrange("p (j w i h e) -> p j w i h e", j=pairs, w=2, h=2, e=RUN)
 
-        def take_odds(r, c):
-            odds[(r, c)] = regrouped.tile([P, CHUNK_K // HALVES], BF16, name="odd_halves")
-            pairs = CHUNK_PASSES // PAIR
+        def loaded(r, g, n):
+            c = set_of[g]
+            first = (g - first_pass[c]) * K_PASS
+            return split(raw[(r, c)][:, first : first + n * K_PASS], n // PAIR)
+
+        def take_odds(r, g, n):
+            odds[(r, g)] = regrouped.tile([P, REGROUP_PASSES * K_PASS // HALVES], BF16, name="odd_halves")
+            target = odds[(r, g)][:, : n * K_PASS // HALVES]
             nc.vector.tensor_copy(
-                out=odds[(r, c)][:].rearrange("p (j i w e) -> p j w i e", j=pairs, w=2, e=RUN),
-                in_=split(raw[(r, c)][:], pairs)[:, :, :, :, 1, :],
+                out=target.rearrange("p (j i w e) -> p j w i e", j=n // PAIR, w=2, e=RUN),
+                in_=loaded(r, g, n)[:, :, :, :, 1, :],
             )
 
-        def move_evens(r, c):
-            halves = split(raw[(r, c)][:], CHUNK_PASSES // PAIR)
+        def move_evens(r, g, n):
+            halves = loaded(r, g, n)
             nc.vector.tensor_copy(out=halves[:, :, 0, :, 1, :], in_=halves[:, :, 1, :, 0, :])
 
         w_codes = consts.tile([P, PASSES, F_OUT], U32, name="w_codes", align_bytes=64)
         w_scales = consts.tile([P, PASSES, F_OUT], U8, name="w_scales", align_bytes=64)
         units = []
-        for c in range(CHUNKS):
-            passes = range(c * CHUNK_PASSES, (c + 1) * CHUNK_PASSES)
+        for c, n_passes in enumerate(SET_PASSES):
+            passes = range(first_pass[c], first_pass[c] + n_passes)
             for g in passes:
                 units.append([(r, g) for r in W_TILES])
             for r in X_TILES:
                 for g in passes[::SLOTS]:
                     units.append([(r, g + a) for a in range(SLOTS)])
         jobs = []
-        wanted = set()
         for n, slots in enumerate(units):
             for r, g in slots:
-                if (r, g // CHUNK_PASSES) not in wanted:
-                    wanted.add((r, g // CHUNK_PASSES))
-                    jobs.append((n, r, g // CHUNK_PASSES))
+                if (r, g) not in job_of:
+                    c = set_of[g]
+                    n_passes = min(REGROUP_PASSES, first_pass[c] + SET_PASSES[c] - g)
+                    for a in range(n_passes):
+                        job_of[(r, g + a)] = g
+                    jobs.append((n, r, g, n_passes))
 
         def transpose(slots):
             bank = banks.tile([P, SLOTS, HALVES, P], F32, name="bank")
             for a, (r, g) in enumerate(slots):
-                chunk = (r, g // CHUNK_PASSES)
-                pair, m = divmod(g % CHUNK_PASSES, PAIR)
-                evens = raw[chunk][:].bitcast(F32)
+                pair, m = divmod(g - first_pass[set_of[g]], PAIR)
+                words = raw[(r, set_of[g])][:].bitcast(F32)
                 first = (HALVES * PAIR * pair + m) * P
-                nc.tensor.transpose(bank[:, a, 0, :], evens[:, first : first + P], ident[:])
-                words = odds[chunk][:].bitcast(F32)
-                first = (PAIR * pair + m) * P
+                nc.tensor.transpose(bank[:, a, 0, :], words[:, first : first + P], ident[:])
+                job = job_of[(r, g)]
+                words = odds[(r, job)][:].bitcast(F32)
+                first = (g - job) * P
                 nc.tensor.transpose(bank[:, a, 1, :], words[:, first : first + P], ident[:])
             return bank
 
@@ -174,9 +190,10 @@ def tile_minerva_detex_pa_k_kernel(tc, features, ex_features, gW, gb, out_0, out
 
         issued = []
 
-        def multiply(up_to):
-            while len(issued) < len(products) and products[len(issued)][0] <= up_to:
-                n, r, g, codes, scales = products[len(issued)]
+        def multiply(up_to, at_most):
+            for n, r, g, codes, scales in products[len(issued) : len(issued) + at_most]:
+                if n > up_to:
+                    break
                 issued.append(n)
                 nc.tensor.matmul_mx(
                     out=acc[r],
@@ -191,7 +208,7 @@ def tile_minerva_detex_pa_k_kernel(tc, features, ex_features, gW, gb, out_0, out
         done = 0
         copied = None
         for n, slots in enumerate(units):
-            while len(raw) < min(len(loads), load_index[(slots[0][0], slots[0][1] // CHUNK_PASSES)] + CHUNKS_AHEAD):
+            while len(raw) < min(len(loads), load_index[(slots[0][0], set_of[slots[0][1]])] + CHUNKS_AHEAD):
                 load_next()
             while done < len(jobs) and jobs[done][0] <= n:
                 take_odds(*jobs[done][1:])
@@ -209,11 +226,11 @@ def tile_minerva_detex_pa_k_kernel(tc, features, ex_features, gW, gb, out_0, out
             codes, scales = operand(n, slots)
             copied = (grouped, codes, scales)
             if n % MULTIPLY_EVERY == MULTIPLY_EVERY - 1:
-                multiply(n - MULTIPLY_BEHIND)
+                multiply(n - MULTIPLY_BEHIND, MULTIPLY_RUN)
             if n == MULTIPLY_BEHIND:
                 spread_bias()
         quantise(*copied)
-        multiply(len(units))
+        multiply(len(units), len(products))
 
         y = {}
         groups = [X_TILES[:-1], X_TILES[-1:]]
@@ -222,7 +239,7 @@ def tile_minerva_detex_pa_k_kernel(tc, features, ex_features, gW, gb, out_0, out
             for i, r in enumerate(group):
                 y[r] = tail.tile([P, F_OUT], F32, name="y")
                 nc.vector.tensor_tensor(out=y[r][:], in0=acc[r], in1=bias[:], op=ALU.add)
-                squares = tail.tile([P, F_OUT], F32, name="squares")
+                squares = thrown.tile([P, F_OUT], F32, name="squares")
                 nc.scalar.activation(
                     out=squares[:], in_=y[r][:], func=ACT.Square, accum_out=sum_sq[:, i : i + 1]
                 )
@@ -235,8 +252,5 @@ def tile_minerva_detex_pa_k_kernel(tc, features, ex_features, gW, gb, out_0, out
             inverses.append(inverse)
         for group, inverse in zip(groups, inverses):
             for i, r in enumerate(group):
-                normalised = tail.tile([P, F_OUT], F32, name="normalised")
-                nc.vector.tensor_scalar_mul(
-                    out=normalised[:], in0=y[r][:], scalar1=inverse[:, i : i + 1]
-                )
-                nc.sync.dma_start(out=out_of[r], in_=normalised[:])
+                nc.vector.tensor_scalar_mul(out=y[r][:], in0=y[r][:], scalar1=inverse[:, i : i + 1])
+                nc.sync.dma_start(out=out_of[r], in_=y[r][:])

@@ -22,7 +22,7 @@ K_PASS = PACK * P
 PASSES = K // K_PASS
 HALVES = 2
 SLOTS = 2
-SET_PASSES = (2, 6, 8, 8, 4, 4)
+SET_PASSES = (4,) * 8
 LONGEST = max(SET_PASSES)
 RUN = 16
 PAIR = 2
@@ -32,12 +32,12 @@ W_TILES = (0, 1)
 X_TILES = (2, 3, 4, 5, 6)
 ACC_BANKS = 3
 TRANSPOSE_BANKS = 8 - ACC_BANKS
-CHUNKS_AHEAD = 8
-REGROUP_AHEAD = 10
+CHUNKS_AHEAD = 14
+REGROUP_AHEAD = 8
 REGROUP_PASSES = 4
-MULTIPLY_EVERY = 6
+MULTIPLY_EVERY = 4
 MULTIPLY_BEHIND = 9
-MULTIPLY_RUN = 9
+MULTIPLY_RUN = 6
 
 FLOPS = 2 * (1 + EX_TILES) * P * F_OUT * K
 
@@ -53,7 +53,7 @@ def tile_minerva_detex_pa_k_kernel(tc, features, ex_features, gW, gb, out_0, out
     with ExitStack() as ctx:
         ctx.enter_context(tc.manual_schedule())
         consts = ctx.enter_context(tc.tile_pool(name="consts", bufs=1))
-        raws = ctx.enter_context(tc.tile_pool(name="raws", bufs=12))
+        raws = ctx.enter_context(tc.tile_pool(name="raws", bufs=24))
         regrouped = ctx.enter_context(tc.tile_pool(name="regrouped", bufs=14))
         stage = ctx.enter_context(tc.tile_pool(name="stage", bufs=8))
         xq = ctx.enter_context(tc.tile_pool(name="xq", bufs=24))

@@ -34,10 +34,9 @@ ACC_BANKS = 3
 TRANSPOSE_BANKS = 8 - ACC_BANKS
 CHUNKS_AHEAD = 14
 REGROUP_AHEAD = 8
-REGROUP_PASSES = 4
-MULTIPLY_EVERY = 4
-MULTIPLY_BEHIND = 9
-MULTIPLY_RUN = 6
+MULTIPLY_EVERY = 5
+MULTIPLY_BEHIND = 7
+MULTIPLY_RUN = 8
 
 FLOPS = 2 * (1 + EX_TILES) * P * F_OUT * K
 
@@ -62,22 +61,38 @@ def tile_minerva_detex_pa_k_kernel(tc, features, ex_features, gW, gb, out_0, out
         banks = ctx.enter_context(tc.psum_pool(name="banks", bufs=TRANSPOSE_BANKS))
         accs = ctx.enter_context(tc.psum_pool(name="accs", bufs=ACC_BANKS))
 
+        bias_row = consts.tile([P, F_OUT], BF16, name="bias_row")
+        nc.vector.memset(bias_row[:], 0.0)
+        nc.scalar.dma_start(out=bias_row[0:1, :], in_=gb.rearrange("(o f) -> o f", o=1))
+
         first_pass = [sum(SET_PASSES[:c]) for c in range(len(SET_PASSES))]
         set_of = {}
         for c, n in enumerate(SET_PASSES):
             for g in range(first_pass[c], first_pass[c] + n):
                 set_of[g] = c
-        loads = [(r, c) for c in range(len(SET_PASSES)) for r in W_TILES + X_TILES]
-        load_index = {}
+        pieces = []
+        for g in range(0, SET_PASSES[0], PAIR):
+            pieces += [(r, g, PAIR) for r in W_TILES]
+        pieces += [(r, 0, SET_PASSES[0]) for r in X_TILES]
+        for g, n in list(zip(first_pass, SET_PASSES))[1:]:
+            pieces += [(r, g, n) for r in W_TILES + X_TILES]
+        piece_of = {}
+        for i, (r, g, n) in enumerate(pieces):
+            for a in range(n):
+                piece_of[(r, g + a)] = i
         raw = {}
+        loaded_pieces = []
 
         def load_next():
-            r, c = loads[len(raw)]
-            load_index[(r, c)] = len(raw)
-            raw[(r, c)] = raws.tile([P, LONGEST * K_PASS], BF16, name="chunk")
-            k = slice(first_pass[c] * K_PASS, (first_pass[c] + SET_PASSES[c]) * K_PASS)
+            r, g, n = pieces[len(loaded_pieces)]
+            loaded_pieces.append(g)
+            c = set_of[g]
+            if g == first_pass[c]:
+                raw[(r, c)] = raws.tile([P, LONGEST * K_PASS], BF16, name="chunk")
+            k = (g - first_pass[c]) * K_PASS
             nc.sync.dma_start(
-                out=raw[(r, c)][:, : SET_PASSES[c] * K_PASS], in_=rows_of[r][:, k]
+                out=raw[(r, c)][:, k : k + n * K_PASS],
+                in_=rows_of[r][:, g * K_PASS : (g + n) * K_PASS],
             )
 
         for ahead in range(CHUNKS_AHEAD):
@@ -86,17 +101,11 @@ def tile_minerva_detex_pa_k_kernel(tc, features, ex_features, gW, gb, out_0, out
         ident = consts.tile([P, P], F32, name="ident")
         masks.make_identity(nc, ident[:])
 
-        bias_row = consts.tile([P, F_OUT], BF16, name="bias_row")
-        nc.vector.memset(bias_row[:], 0.0)
-        nc.scalar.dma_start(out=bias_row[0:1, :], in_=gb.rearrange("(o f) -> o f", o=1))
         ones = consts.tile([P, P], BF16, name="ones")
         nc.vector.memset(ones[:], 1.0)
         bias = consts.tile([P, F_OUT], F32, name="bias")
-
-        def spread_bias():
-            bias_bank = banks.tile([P, F_OUT], F32, name="bias_bank", tag="bank")
-            nc.tensor.matmul(out=bias_bank[:], lhsT=ones[:], rhs=bias_row[:], start=True, stop=True)
-            nc.vector.tensor_copy(out=bias[:], in_=bias_bank[:])
+        acc_bank = [accs.tile([P, 2, F_OUT], F32, name="acc") for b in range(ACC_BANKS)]
+        bias_bank = acc_bank[-1][:, 0, :]
 
         one = consts.tile([P, 1], F32, name="one")
         nc.vector.memset(one[:], 1.0)
@@ -104,7 +113,6 @@ def tile_minerva_detex_pa_k_kernel(tc, features, ex_features, gW, gb, out_0, out
         nc.scalar.activation(out=one_root[:], in_=one[:], func=ACT.Abs_reciprocal_sqrt)
 
         odds = {}
-        job_of = {}
 
         def split(view, pairs):
             return view.rearrange("p (j w i h e) -> p j w i h e", j=pairs, w=2, h=2, e=RUN)
@@ -115,7 +123,7 @@ def tile_minerva_detex_pa_k_kernel(tc, features, ex_features, gW, gb, out_0, out
             return split(raw[(r, c)][:, first : first + n * K_PASS], n // PAIR)
 
         def take_odds(r, g, n):
-            odds[(r, g)] = regrouped.tile([P, REGROUP_PASSES * K_PASS // HALVES], BF16, name="odd_halves")
+            odds[(r, g)] = regrouped.tile([P, LONGEST * K_PASS // HALVES], BF16, name="odd_halves")
             target = odds[(r, g)][:, : n * K_PASS // HALVES]
             nc.vector.tensor_copy(
                 out=target.rearrange("p (j i w e) -> p j w i e", j=n // PAIR, w=2, e=RUN),
@@ -139,12 +147,9 @@ def tile_minerva_detex_pa_k_kernel(tc, features, ex_features, gW, gb, out_0, out
         jobs = []
         for n, slots in enumerate(units):
             for r, g in slots:
-                if (r, g) not in job_of:
-                    c = set_of[g]
-                    n_passes = min(REGROUP_PASSES, first_pass[c] + SET_PASSES[c] - g)
-                    for a in range(n_passes):
-                        job_of[(r, g + a)] = g
-                    jobs.append((n, r, g, n_passes))
+                piece = pieces[piece_of[(r, g)]]
+                if piece[1] == g:
+                    jobs.append((n, *piece))
 
         def transpose(slots):
             bank = banks.tile([P, SLOTS, HALVES, P], F32, name="bank")
@@ -153,15 +158,15 @@ def tile_minerva_detex_pa_k_kernel(tc, features, ex_features, gW, gb, out_0, out
                 words = raw[(r, set_of[g])][:].bitcast(F32)
                 first = (HALVES * PAIR * pair + m) * P
                 nc.tensor.transpose(bank[:, a, 0, :], words[:, first : first + P], ident[:])
-                job = job_of[(r, g)]
+                job = pieces[piece_of[(r, g)]][1]
                 words = odds[(r, job)][:].bitcast(F32)
                 first = (g - job) * P
                 nc.tensor.transpose(bank[:, a, 1, :], words[:, first : first + P], ident[:])
             return bank
 
-        def interleave(bank):
+        def interleave(bank, copy):
             grouped = stage.tile([P, SLOTS * P * PACK], BF16, name="grouped", align_bytes=64)
-            nc.scalar.copy(
+            copy(
                 out=grouped[:].bitcast(F32).rearrange("p (a r u) -> p a r u", a=SLOTS, u=HALVES),
                 in_=bank[:].rearrange("p a u r -> p a r u"),
             )
@@ -183,7 +188,6 @@ def tile_minerva_detex_pa_k_kernel(tc, features, ex_features, gW, gb, out_0, out
         def quantise(grouped, codes, scales):
             nc.vector.quantize_mx(out=codes.bitcast(FP8X4), scales=scales, in_=grouped[:])
 
-        acc_bank = [accs.tile([P, 2, F_OUT], F32, name="acc") for b in range(ACC_BANKS)]
         acc = {r: acc_bank[i // 2][:, i % 2, :] for i, r in enumerate(X_TILES)}
         opens = X_TILES[0::2]
         closes = X_TILES[1::2] + X_TILES[-1:]
@@ -205,16 +209,31 @@ def tile_minerva_detex_pa_k_kernel(tc, features, ex_features, gW, gb, out_0, out
                     stop=(g == PASSES - 1 and r in closes),
                 )
 
+        y = {}
+        groups = [X_TILES[:-1], X_TILES[-1:]]
+        group_sums = [tail.tile([P, len(group)], F32, name="sum_sq") for group in groups]
+        sum_of = {}
+        for group, sum_sq in zip(groups, group_sums):
+            for i, r in enumerate(group):
+                sum_of[r] = sum_sq[:, i : i + 1]
+
+        def add_bias_and_square(r):
+            y[r] = tail.tile([P, F_OUT], F32, name="y")
+            nc.vector.tensor_tensor(out=y[r][:], in0=acc[r], in1=bias[:], op=ALU.add)
+            squares = thrown.tile([P, F_OUT], F32, name="squares")
+            nc.scalar.activation(out=squares[:], in_=y[r][:], func=ACT.Square, accum_out=sum_of[r])
+
         done = 0
         copied = None
         for n, slots in enumerate(units):
-            while len(raw) < min(len(loads), load_index[(slots[0][0], set_of[slots[0][1]])] + CHUNKS_AHEAD):
+            while len(loaded_pieces) < min(len(pieces), piece_of[slots[0]] + CHUNKS_AHEAD):
                 load_next()
             while done < len(jobs) and jobs[done][0] <= n:
                 take_odds(*jobs[done][1:])
                 move_evens(*jobs[done][1:])
                 done += 1
-            grouped = interleave(transpose(slots))
+            last = n == len(units) - 1
+            grouped = interleave(transpose(slots), nc.vector.tensor_copy if last else nc.scalar.copy)
             begun = done < len(jobs) and jobs[done][0] <= n + REGROUP_AHEAD
             if begun:
                 take_odds(*jobs[done][1:])
@@ -227,30 +246,30 @@ def tile_minerva_detex_pa_k_kernel(tc, features, ex_features, gW, gb, out_0, out
             copied = (grouped, codes, scales)
             if n % MULTIPLY_EVERY == MULTIPLY_EVERY - 1:
                 multiply(n - MULTIPLY_BEHIND, MULTIPLY_RUN)
-            if n == MULTIPLY_BEHIND:
-                spread_bias()
+            if n == 2:
+                nc.tensor.matmul(out=bias_bank, lhsT=ones[:], rhs=bias_row[:], start=True, stop=True)
+                nc.vector.tensor_copy(out=bias[:], in_=bias_bank)
         quantise(*copied)
         multiply(len(units), len(products))
 
-        y = {}
-        groups = [X_TILES[:-1], X_TILES[-1:]]
-        group_sums = [tail.tile([P, len(group)], F32, name="sum_sq") for group in groups]
-        for group, sum_sq in zip(groups, group_sums):
-            for i, r in enumerate(group):
-                y[r] = tail.tile([P, F_OUT], F32, name="y")
-                nc.vector.tensor_tensor(out=y[r][:], in0=acc[r], in1=bias[:], op=ALU.add)
-                squares = thrown.tile([P, F_OUT], F32, name="squares")
-                nc.scalar.activation(
-                    out=squares[:], in_=y[r][:], func=ACT.Square, accum_out=sum_sq[:, i : i + 1]
-                )
-        inverses = []
-        for group, sum_sq in zip(groups, group_sums):
-            clamped = tail.tile([P, len(group)], F32, name="clamped")
-            nc.vector.tensor_scalar_max(out=clamped[:], in0=sum_sq[:], scalar1=EPS * EPS)
-            inverse = tail.tile([P, len(group)], F32, name="inverse")
-            nc.scalar.activation(out=inverse[:], in_=clamped[:], func=ACT.Abs_reciprocal_sqrt)
-            inverses.append(inverse)
-        for group, inverse in zip(groups, inverses):
-            for i, r in enumerate(group):
-                nc.vector.tensor_scalar_mul(out=y[r][:], in0=y[r][:], scalar1=inverse[:, i : i + 1])
+        for r in X_TILES[:-1]:
+            add_bias_and_square(r)
+        inverses = {}
+
+        def invert(i):
+            clamped = tail.tile([P, len(groups[i])], F32, name="clamped")
+            nc.vector.tensor_scalar_max(out=clamped[:], in0=group_sums[i][:], scalar1=EPS * EPS)
+            inverses[i] = tail.tile([P, len(groups[i])], F32, name="inverse")
+            nc.scalar.activation(out=inverses[i][:], in_=clamped[:], func=ACT.Abs_reciprocal_sqrt)
+
+        def scale_and_store(i):
+            for j, r in enumerate(groups[i]):
+                inverse = inverses[i][:, j : j + 1]
+                nc.vector.tensor_scalar_mul(out=y[r][:], in0=y[r][:], scalar1=inverse)
                 nc.sync.dma_start(out=out_of[r], in_=y[r][:])
+
+        add_bias_and_square(X_TILES[-1])
+        for i in range(len(groups)):
+            invert(i)
+        for i in range(len(groups)):
+            scale_and_store(i)

@@ -34,9 +34,9 @@ ACC_BANKS = 3
 TRANSPOSE_BANKS = 8 - ACC_BANKS
 CHUNKS_AHEAD = 14
 REGROUP_AHEAD = 8
-MULTIPLY_EVERY = 5
-MULTIPLY_BEHIND = 7
-MULTIPLY_RUN = 8
+MULTIPLY_EVERY = 4
+MULTIPLY_BEHIND = 6
+WARM_UP = 5
 
 FLOPS = 2 * (1 + EX_TILES) * P * F_OUT * K
 
@@ -106,6 +106,15 @@ def tile_minerva_detex_pa_k_kernel(tc, features, ex_features, gW, gb, out_0, out
         bias = consts.tile([P, F_OUT], F32, name="bias")
         acc_bank = [accs.tile([P, 2, F_OUT], F32, name="acc") for b in range(ACC_BANKS)]
         bias_bank = acc_bank[-1][:, 0, :]
+        some = consts.tile([P, 2 * F_OUT], BF16, name="some")
+        nc.gpsimd.memset(some[:], 1.0)
+
+        def warm(columns):
+            bank = acc_bank[0][:].rearrange("p a f -> p (a f)")
+            nc.tensor.matmul(
+                out=bank[:, :columns], lhsT=ones[:], rhs=some[:, :columns], start=True, stop=True
+            )
+
 
         one = consts.tile([P, 1], F32, name="one")
         nc.vector.memset(one[:], 1.0)
@@ -194,10 +203,8 @@ def tile_minerva_detex_pa_k_kernel(tc, features, ex_features, gW, gb, out_0, out
 
         issued = []
 
-        def multiply(up_to, at_most):
-            for n, r, g, codes, scales in products[len(issued) : len(issued) + at_most]:
-                if n > up_to:
-                    break
+        def multiply(due):
+            for n, r, g, codes, scales in products[len(issued) : due]:
                 issued.append(n)
                 nc.tensor.matmul_mx(
                     out=acc[r],
@@ -223,6 +230,11 @@ def tile_minerva_detex_pa_k_kernel(tc, features, ex_features, gW, gb, out_0, out
             squares = thrown.tile([P, F_OUT], F32, name="squares")
             nc.scalar.activation(out=squares[:], in_=y[r][:], func=ACT.Square, accum_out=sum_of[r])
 
+        per_set = len(X_TILES) * LONGEST
+        units_per_set = LONGEST + len(X_TILES) * LONGEST // SLOTS
+        first_due = LONGEST + MULTIPLY_BEHIND - 1
+        for i in range(WARM_UP):
+            warm(2 * F_OUT)
         done = 0
         copied = None
         for n, slots in enumerate(units):
@@ -244,13 +256,16 @@ def tile_minerva_detex_pa_k_kernel(tc, features, ex_features, gW, gb, out_0, out
                 done += 1
             codes, scales = operand(n, slots)
             copied = (grouped, codes, scales)
-            if n % MULTIPLY_EVERY == MULTIPLY_EVERY - 1:
-                multiply(n - MULTIPLY_BEHIND, MULTIPLY_RUN)
+            due = (n - first_due) * per_set // units_per_set
+            if due <= 0:
+                warm(F_OUT)
+            elif n % MULTIPLY_EVERY == MULTIPLY_EVERY - 1:
+                multiply(due)
             if n == 2:
                 nc.tensor.matmul(out=bias_bank, lhsT=ones[:], rhs=bias_row[:], start=True, stop=True)
                 nc.vector.tensor_copy(out=bias[:], in_=bias_bank)
         quantise(*copied)
-        multiply(len(units), len(products))
+        multiply(len(units) * SLOTS)
 
         for r in X_TILES[:-1]:
             add_bias_and_square(r)

@@ -52,9 +52,9 @@ def tile_minerva_detex_pa_k_kernel(tc, features, ex_features, gW, gb, out_0, out
     with ExitStack() as ctx:
         ctx.enter_context(tc.manual_schedule())
         consts = ctx.enter_context(tc.tile_pool(name="consts", bufs=1))
-        raws = ctx.enter_context(tc.tile_pool(name="raws", bufs=24))
+        raws = ctx.enter_context(tc.tile_pool(name="raws", bufs=19))
         regrouped = ctx.enter_context(tc.tile_pool(name="regrouped", bufs=14))
-        stage = ctx.enter_context(tc.tile_pool(name="stage", bufs=8))
+        stage = ctx.enter_context(tc.tile_pool(name="stage", bufs=18))
         xq = ctx.enter_context(tc.tile_pool(name="xq", bufs=24))
         tail = ctx.enter_context(tc.tile_pool(name="tail", bufs=len(X_TILES)))
         thrown = ctx.enter_context(tc.tile_pool(name="thrown", bufs=2))
@@ -173,9 +173,9 @@ def tile_minerva_detex_pa_k_kernel(tc, features, ex_features, gW, gb, out_0, out
                 nc.tensor.transpose(bank[:, a, 1, :], words[:, first : first + P], ident[:])
             return bank
 
-        def interleave(bank, copy):
+        def interleave(bank):
             grouped = stage.tile([P, SLOTS * P * PACK], BF16, name="grouped", align_bytes=64)
-            copy(
+            nc.scalar.copy(
                 out=grouped[:].bitcast(F32).rearrange("p (a r u) -> p a r u", a=SLOTS, u=HALVES),
                 in_=bank[:].rearrange("p a u r -> p a r u"),
             )
@@ -217,7 +217,7 @@ def tile_minerva_detex_pa_k_kernel(tc, features, ex_features, gW, gb, out_0, out
                 )
 
         y = {}
-        groups = [X_TILES[:-1], X_TILES[-1:]]
+        groups = [X_TILES[:2], X_TILES[2:]]
         group_sums = [tail.tile([P, len(group)], F32, name="sum_sq") for group in groups]
         sum_of = {}
         for group, sum_sq in zip(groups, group_sums):
@@ -244,8 +244,7 @@ def tile_minerva_detex_pa_k_kernel(tc, features, ex_features, gW, gb, out_0, out
                 take_odds(*jobs[done][1:])
                 move_evens(*jobs[done][1:])
                 done += 1
-            last = n == len(units) - 1
-            grouped = interleave(transpose(slots), nc.vector.tensor_copy if last else nc.scalar.copy)
+            grouped = interleave(transpose(slots))
             begun = done < len(jobs) and jobs[done][0] <= n + REGROUP_AHEAD
             if begun:
                 take_odds(*jobs[done][1:])
@@ -264,10 +263,11 @@ def tile_minerva_detex_pa_k_kernel(tc, features, ex_features, gW, gb, out_0, out
             if n == 2:
                 nc.tensor.matmul(out=bias_bank, lhsT=ones[:], rhs=bias_row[:], start=True, stop=True)
                 nc.vector.tensor_copy(out=bias[:], in_=bias_bank)
+        multiply(len(products) - SLOTS)
+        add_bias_and_square(X_TILES[0])
         quantise(*copied)
-        multiply(len(units) * SLOTS)
-
-        for r in X_TILES[:-1]:
+        multiply(len(products))
+        for r in X_TILES[1:4]:
             add_bias_and_square(r)
         inverses = {}
 
@@ -283,8 +283,8 @@ def tile_minerva_detex_pa_k_kernel(tc, features, ex_features, gW, gb, out_0, out
                 nc.vector.tensor_scalar_mul(out=y[r][:], in0=y[r][:], scalar1=inverse)
                 nc.sync.dma_start(out=out_of[r], in_=y[r][:])
 
-        add_bias_and_square(X_TILES[-1])
-        for i in range(len(groups)):
-            invert(i)
-        for i in range(len(groups)):
-            scale_and_store(i)
+        invert(0)
+        add_bias_and_square(X_TILES[4])
+        scale_and_store(0)
+        invert(1)
+        scale_and_store(1)

from contextlib import ExitStack

import concourse.masks as masks
import concourse.mybir as mybir

F32 = mybir.dt.float32
BF16 = mybir.dt.bfloat16
U32 = mybir.dt.uint32
U8 = mybir.dt.uint8
FP8X4 = mybir.dt.float8_e4m3fn_x4
ACT = mybir.ActivationFunctionType
ALU = mybir.AluOpType

P = 128
K = 16384
F_OUT = 256
EX_TILES = 4
EPS = 1e-12

PACK = 4
K_PASS = PACK * P
PASSES = K // K_PASS
HALVES = 2
SLOTS = 2
SET_PASSES = (4,) * 8
LONGEST = max(SET_PASSES)
RUN = 16
PAIR = 2
PAIR_K = PAIR * K_PASS

W_TILES = (0, 1)
X_TILES = (2, 3, 4, 5, 6)
ACC_BANKS = 3
TRANSPOSE_BANKS = 8 - ACC_BANKS
CHUNKS_AHEAD = 14
REGROUP_AHEAD = 8
MULTIPLY_EVERY = 4
MULTIPLY_BEHIND = 6
WARM_UP = 5

FLOPS = 2 * (1 + EX_TILES) * P * F_OUT * K


def tile_minerva_detex_pa_k_kernel(tc, features, ex_features, gW, gb, out_0, out_1):
    nc = tc.nc
    rows_of = [gW[0:P, :], gW[P : 2 * P, :], features]
    out_of = {2: out_0}
    for i in range(EX_TILES):
        out_of[len(rows_of)] = out_1[i * P : (i + 1) * P, :]
        rows_of.append(ex_features[i * P : (i + 1) * P, :])

    with ExitStack() as ctx:
        ctx.enter_context(tc.manual_schedule())
        consts = ctx.enter_context(tc.tile_pool(name="consts", bufs=1))
        raws = ctx.enter_context(tc.tile_pool(name="raws", bufs=19))
        regrouped = ctx.enter_context(tc.tile_pool(name="regrouped", bufs=14))
        stage = ctx.enter_context(tc.tile_pool(name="stage", bufs=18))
        xq = ctx.enter_context(tc.tile_pool(name="xq", bufs=24))
        tail = ctx.enter_context(tc.tile_pool(name="tail", bufs=len(X_TILES)))
        thrown = ctx.enter_context(tc.tile_pool(name="thrown", bufs=2))
        banks = ctx.enter_context(tc.psum_pool(name="banks", bufs=TRANSPOSE_BANKS))
        accs = ctx.enter_context(tc.psum_pool(name="accs", bufs=ACC_BANKS))

        bias_row = consts.tile([P, F_OUT], BF16, name="bias_row")
        nc.vector.memset(bias_row[:], 0.0)
        nc.scalar.dma_start(out=bias_row[0:1, :], in_=gb.rearrange("(o f) -> o f", o=1))

        first_pass = [sum(SET_PASSES[:c]) for c in range(len(SET_PASSES))]
        set_of = {}
        for c, n in enumerate(SET_PASSES):
            for g in range(first_pass[c], first_pass[c] + n):
                set_of[g] = c
        pieces = []
        for g in range(0, SET_PASSES[0], PAIR):
            pieces += [(r, g, PAIR) for r in W_TILES]
        pieces += [(r, 0, SET_PASSES[0]) for r in X_TILES]
        for g, n in list(zip(first_pass, SET_PASSES))[1:]:
            pieces += [(r, g, n) for r in W_TILES + X_TILES]
        piece_of = {}
        for i, (r, g, n) in enumerate(pieces):
            for a in range(n):
                piece_of[(r, g + a)] = i
        raw = {}
        loaded_pieces = []

        def load_next():
            r, g, n = pieces[len(loaded_pieces)]
            loaded_pieces.append(g)
            c = set_of[g]
            if g == first_pass[c]:
                raw[(r, c)] = raws.tile([P, LONGEST * K_PASS], BF16, name="chunk")
            k = (g - first_pass[c]) * K_PASS
            nc.sync.dma_start(
                out=raw[(r, c)][:, k : k + n * K_PASS],
                in_=rows_of[r][:, g * K_PASS : (g + n) * K_PASS],
            )

        for ahead in range(CHUNKS_AHEAD):
            load_next()

        ident = consts.tile([P, P], F32, name="ident")
        masks.make_identity(nc, ident[:])

        ones = consts.tile([P, P], BF16, name="ones")
        nc.vector.memset(ones[:], 1.0)
        bias = consts.tile([P, F_OUT], F32, name="bias")
        acc_bank = [accs.tile([P, 2, F_OUT], F32, name="acc") for b in range(ACC_BANKS)]
        bias_bank = acc_bank[-1][:, 0, :]
        some = consts.tile([P, 2 * F_OUT], BF16, name="some")
        nc.gpsimd.memset(some[:], 1.0)

        def warm(columns):
            bank = acc_bank[0][:].rearrange("p a f -> p (a f)")
            nc.tensor.matmul(
                out=bank[:, :columns], lhsT=ones[:], rhs=some[:, :columns], start=True, stop=True
            )


        one = consts.tile([P, 1], F32, name="one")
        nc.vector.memset(one[:], 1.0)
        one_root = consts.tile([P, 1], F32, name="one_root")
        nc.scalar.activation(out=one_root[:], in_=one[:], func=ACT.Abs_reciprocal_sqrt)

        odds = {}

        def split(view, pairs):
            return view.rearrange("p (j w i h e) -> p j w i h e", j=pairs, w=2, h=2, e=RUN)

        def loaded(r, g, n):
            c = set_of[g]
            first = (g - first_pass[c]) * K_PASS
            return split(raw[(r, c)][:, first : first + n * K_PASS], n // PAIR)

        def take_odds(r, g, n):
            odds[(r, g)] = regrouped.tile([P, LONGEST * K_PASS // HALVES], BF16, name="odd_halves")
            target = odds[(r, g)][:, : n * K_PASS // HALVES]
            nc.vector.tensor_copy(
                out=target.rearrange("p (j i w e) -> p j w i e", j=n // PAIR, w=2, e=RUN),
                in_=loaded(r, g, n)[:, :, :, :, 1, :],
            )

        def move_evens(r, g, n):
            halves = loaded(r, g, n)
            nc.vector.tensor_copy(out=halves[:, :, 0, :, 1, :], in_=halves[:, :, 1, :, 0, :])

        w_codes = consts.tile([P, PASSES, F_OUT], U32, name="w_codes", align_bytes=64)
        w_scales = consts.tile([P, PASSES, F_OUT], U8, name="w_scales", align_bytes=64)
        units = []
        for c, n_passes in enumerate(SET_PASSES):
            passes = range(first_pass[c], first_pass[c] + n_passes)
            for g in passes:
                units.append([(r, g) for r in W_TILES])
            for r in X_TILES:
                for g in passes[::SLOTS]:
                    units.append([(r, g + a) for a in range(SLOTS)])
        jobs = []
        for n, slots in enumerate(units):
            for r, g in slots:
                piece = pieces[piece_of[(r, g)]]
                if piece[1] == g:
                    jobs.append((n, *piece))

        def transpose(slots):
            bank = banks.tile([P, SLOTS, HALVES, P], F32, name="bank")
            for a, (r, g) in enumerate(slots):
                pair, m = divmod(g - first_pass[set_of[g]], PAIR)
                words = raw[(r, set_of[g])][:].bitcast(F32)
                first = (HALVES * PAIR * pair + m) * P
                nc.tensor.transpose(bank[:, a, 0, :], words[:, first : first + P], ident[:])
                job = pieces[piece_of[(r, g)]][1]
                words = odds[(r, job)][:].bitcast(F32)
                first = (g - job) * P
                nc.tensor.transpose(bank[:, a, 1, :], words[:, first : first + P], ident[:])
            return bank

        def interleave(bank):
            grouped = stage.tile([P, SLOTS * P * PACK], BF16, name="grouped", align_bytes=64)
            nc.scalar.copy(
                out=grouped[:].bitcast(F32).rearrange("p (a r u) -> p a r u", a=SLOTS, u=HALVES),
                in_=bank[:].rearrange("p a u r -> p a r u"),
            )
            return grouped

        products = []

        def operand(n, slots):
            if slots[0][0] in W_TILES:
                g = slots[0][1]
                return w_codes[:, g, :], w_scales[:, g, :]
            codes = xq.tile([P, SLOTS * P], U32, name="x_codes", align_bytes=64)
            scales = xq.tile([P, SLOTS * P], U8, name="x_scales", align_bytes=64)
            for a, (r, g) in enumerate(slots):
                cols = slice(a * P, (a + 1) * P)
                products.append((n, r, g, codes[:, cols], scales[:, cols]))
            return codes[:], scales[:]

        def quantise(grouped, codes, scales):
            nc.vector.quantize_mx(out=codes.bitcast(FP8X4), scales=scales, in_=grouped[:])

        acc = {r: acc_bank[i // 2][:, i % 2, :] for i, r in enumerate(X_TILES)}
        opens = X_TILES[0::2]
        closes = X_TILES[1::2] + X_TILES[-1:]

        issued = []

        def multiply(due):
            for n, r, g, codes, scales in products[len(issued) : due]:
                issued.append(n)
                nc.tensor.matmul_mx(
                    out=acc[r],
                    lhsT=codes.bitcast(FP8X4),
                    lhsT_scale=scales,
                    rhs=w_codes[:, g, :].bitcast(FP8X4),
                    rhs_scale=w_scales[:, g, :],
                    start=(g == 0 and r in opens),
                    stop=(g == PASSES - 1 and r in closes),
                )

        y = {}
        groups = [X_TILES[:2], X_TILES[2:]]
        group_sums = [tail.tile([P, len(group)], F32, name="sum_sq") for group in groups]
        sum_of = {}
        for group, sum_sq in zip(groups, group_sums):
            for i, r in enumerate(group):
                sum_of[r] = sum_sq[:, i : i + 1]

        def add_bias_and_square(r):
            y[r] = tail.tile([P, F_OUT], F32, name="y")
            nc.vector.tensor_tensor(out=y[r][:], in0=acc[r], in1=bias[:], op=ALU.add)
            squares = thrown.tile([P, F_OUT], F32, name="squares")
            nc.scalar.activation(out=squares[:], in_=y[r][:], func=ACT.Square, accum_out=sum_of[r])

        per_set = len(X_TILES) * LONGEST
        units_per_set = LONGEST + len(X_TILES) * LONGEST // SLOTS
        first_due = LONGEST + MULTIPLY_BEHIND - 1
        for i in range(WARM_UP):
            warm(2 * F_OUT)
        done = 0
        copied = None
        for n, slots in enumerate(units):
            while len(loaded_pieces) < min(len(pieces), piece_of[slots[0]] + CHUNKS_AHEAD):
                load_next()
            while done < len(jobs) and jobs[done][0] <= n:
                take_odds(*jobs[done][1:])
                move_evens(*jobs[done][1:])
                done += 1
            grouped = interleave(transpose(slots))
            begun = done < len(jobs) and jobs[done][0] <= n + REGROUP_AHEAD
            if begun:
                take_odds(*jobs[done][1:])
            if copied is not None:
                quantise(*copied)
            if begun:
                move_evens(*jobs[done][1:])
                done += 1
            codes, scales = operand(n, slots)
            copied = (grouped, codes, scales)
            due = (n - first_due) * per_set // units_per_set
            if due <= 0:
                warm(F_OUT)
            elif n % MULTIPLY_EVERY == MULTIPLY_EVERY - 1:
                multiply(due)
            if n == 2:
                nc.tensor.matmul(out=bias_bank, lhsT=ones[:], rhs=bias_row[:], start=True, stop=True)
                nc.vector.tensor_copy(out=bias[:], in_=bias_bank)
        multiply(len(products) - SLOTS)
        add_bias_and_square(X_TILES[0])
        quantise(*copied)
        multiply(len(products))
        for r in X_TILES[1:4]:
            add_bias_and_square(r)
        inverses = {}

        def invert(i):
            clamped = tail.tile([P, len(groups[i])], F32, name="clamped")
            nc.vector.tensor_scalar_max(out=clamped[:], in0=group_sums[i][:], scalar1=EPS * EPS)
            inverses[i] = tail.tile([P, len(groups[i])], F32, name="inverse")
            nc.scalar.activation(out=inverses[i][:], in_=clamped[:], func=ACT.Abs_reciprocal_sqrt)

        def scale_and_store(i):
            for j, r in enumerate(groups[i]):
                inverse = inverses[i][:, j : j + 1]
                nc.vector.tensor_scalar_mul(out=y[r][:], in0=y[r][:], scalar1=inverse)
                nc.sync.dma_start(out=out_of[r], in_=y[r][:])

        invert(0)
        add_bias_and_square(X_TILES[4])
        scale_and_store(0)
        invert(1)
        scale_and_store(1)
